import numpy as np
import ml_dtypes


def mxq(x, axis, fmt="e4m3"):
    dtype, down = {"e4m3": (ml_dtypes.float8_e4m3fn, 7), "e5m2": (ml_dtypes.float8_e5m2, 14)}[fmt]
    v = np.moveaxis(np.asarray(x, np.float32).astype(ml_dtypes.bfloat16).astype(np.float64), axis, -1)
    blocks = v.reshape(v.shape[:-1] + (-1, 32))
    amax = np.abs(blocks).max(-1, keepdims=True)
    byte = np.maximum(np.where(amax > 0, np.frexp(amax)[1] - 1 + 127, 0) - down, 1)
    scale = np.exp2(byte - 127.0)
    codes = (blocks / scale).astype(np.float32).astype(dtype).astype(np.float64)
    return np.moveaxis((codes * scale).reshape(v.shape), -1, axis)


WIDE = False


def mx_kscale(k):
    if not WIDE:
        return np.ones(k)
    levels = np.array([20, -20, 10, -10, 0])
    a = np.random.permutation(np.resize(levels, k // 512 * 4)).reshape(k // 512, 4)
    idx = np.arange(k)
    return np.exp2(a[idx // 512, idx % 128 // 32])


BF16 = ml_dtypes.bfloat16


def bf(x):
    return np.asarray(x, np.float32).astype(BF16)


def f64(x):
    return np.asarray(x).astype(np.float64)


G, GI, GO, B = 32, 32, 32, 4096
K = G * GI
N = G * GO


def build_mask():
    mask = np.ones((N, K))
    for g in range(G):
        mask[g * GO:(g + 1) * GO, g * GI:(g + 1) * GI] = 0.0
    return mask


def setup_inputs():
    u = mx_kscale(N)
    bound = 1.0 / np.sqrt(K)
    W = np.random.uniform(-bound, bound, (N, K)) * build_mask() / u[:, None]
    data = np.random.standard_normal((B, K))
    b = np.random.standard_normal(N) * 0.3
    g = np.random.standard_normal((B, N)) * np.exp2(np.random.randint(-12, 1, (B, 1))) * 4.0 * u[None, :]
    return {"data": bf(data), "W": bf(W), "b": bf(b), "grad_out": bf(g)}


def reference(data, W, b, grad_out):
    return mxq(f64(grad_out), 1, "e5m2") @ mxq(f64(W), 0, "e4m3")

@@ -1,0 +1,175 @@
+from contextlib import ExitStack
+
+import concourse.masks as masks
+import concourse.mybir as mybir
+
+F32 = mybir.dt.float32
+BF16 = mybir.dt.bfloat16
+U32 = mybir.dt.uint32
+U8 = mybir.dt.uint8
+E4 = mybir.dt.float8_e4m3fn_x4
+E5 = mybir.dt.float8_e5m2_x4
+
+P = 128
+B = 4096
+C = 1024
+N = 1024
+FLOPS = 2 * B * C * N
+BYTES = B * C * 2 + C * N * 2 + B * N * 4
+PINNED = True
+V_COLS = 336
+
+
+def tile_groupfc_t_kernel(tc, data, W, b, grad_out, out):
+    nc = tc.nc
+    with ExitStack() as ctx:
+        if PINNED:
+            ctx.enter_context(tc.manual_schedule())
+        keep = ctx.enter_context(tc.tile_pool(name="keep", bufs=1))
+        grp = ctx.enter_context(tc.tile_pool(name="grp", bufs=3))
+        stg = ctx.enter_context(tc.tile_pool(name="stg", bufs=10))
+        ps = ctx.enter_context(tc.psum_pool(name="ps", bufs=4))
+
+        ident = keep.tile([P, P], F32, name="ident")
+        masks.make_identity(nc, ident[:])
+
+        g_view = [grad_out[512 * m:512 * (m + 1), :].rearrange("(p j) c -> p j c", j=4) for m in range(8)]
+        o_view = [out[512 * m:512 * (m + 1), :].rearrange("(p j) n -> p j n", j=4) for m in range(8)]
+        g_sb = [keep.tile([P, 4, C], BF16, name="g%d" % m) for m in range(8)]
+        w_raw = [keep.tile([P, 4, N], BF16, name="wr%d" % c) for c in range(2)]
+        w_grp = [[keep.tile([P, 512, 4], BF16, name="wg%d%d" % (c, h), align_bytes=64) for h in range(2)] for c in range(2)]
+        w_codes = keep.tile([P, 2, N], U32, name="w_codes", align_bytes=64)
+        w_scales = keep.tile([P, 2, N], U8, name="w_scales", align_bytes=64)
+
+        nc.sync.dma_start(out=g_sb[0][:, 0:2, :], in_=g_view[0][:, 0:2, :])
+        for c in range(2):
+            nc.sync.dma_start(
+                out=w_raw[c][:].rearrange("p (u e) n -> p u (e n)", u=2),
+                in_=W[512 * c:512 * (c + 1), :].rearrange("(u q e) n -> q u (e n)", u=2, e=2),
+            )
+        nc.sync.dma_start(out=g_sb[0][:, 2:4, :], in_=g_view[0][:, 2:4, :])
+        for m in range(1, 8):
+            nc.sync.dma_start(out=g_sb[m][:], in_=g_view[m])
+
+        xts = {}
+        ggs = {}
+        gcs = {}
+        accs = {}
+        sts = {}
+
+        def transposes(pr):
+            words = g_sb[pr // 2][:].bitcast(F32)
+            for a in range(2):
+                xt = ps.tile([P, 4, P], F32, name="xt", tag="xt")
+                xts[(pr, a)] = xt
+                for s in range(4):
+                    nc.tensor.transpose(xt[:, s, :], words[:, 2 * (pr % 2) + a, P * s:P * (s + 1)], ident[:])
+
+        def copies(pr):
+            gg = grp.tile([P, 2, C], BF16, name="gg", tag="gg", align_bytes=64)
+            ggs[pr] = gg
+            ggw = gg[:].bitcast(F32)
+            for a in range(2):
+                dst = ggw[:, a, :].rearrange("p (c r u) -> p c r u", c=2, u=2)
+                src = xts[(pr, a)][:].rearrange("p (c u) r -> p c r u", u=2)
+                if a == 0:
+                    nc.vector.tensor_copy(out=dst, in_=src)
+                else:
+                    nc.scalar.copy(out=dst, in_=src)
+
+        def quantise(pr):
+            gc = grp.tile([P, 512], U32, name="gc", tag="gc", align_bytes=64)
+            gs = grp.tile([P, 512], U8, name="gs", tag="gs", align_bytes=64)
+            gcs[pr] = (gc, gs)
+            nc.vector.quantize_mx(out=gc[:].bitcast(E5), scales=gs[:], in_=ggs[pr][:].rearrange("p a k -> p (a k)"))
+
+        def mx_pass(pr, a, h, c):
+            if c == 0:
+                accs[(pr, a, h)] = ps.tile([P, 512], F32, name="acc", tag="acc")
+            gc, gs = gcs[pr]
+            lo = 256 * a + P * c
+            nc.tensor.matmul_mx(
+                out=accs[(pr, a, h)][:],
+                lhsT=gc[:, lo:lo + P].bitcast(E5),
+                lhsT_scale=gs[:, lo:lo + P],
+                rhs=w_codes[:, c, 512 * h:512 * (h + 1)].bitcast(E4),
+                rhs_scale=w_scales[:, c, 512 * h:512 * (h + 1)],
+                start=(c == 0),
+                stop=(c == 1),
+            )
+
+        def drain(pr, a, h, on_vector):
+            if (a, h) == (0, 0):
+                sts[pr] = stg.tile([P, 2, N], F32, name="st", tag="st")
+            dst = sts[pr][:, a, 512 * h:512 * (h + 1)]
+            if on_vector:
+                nc.vector.tensor_copy(out=dst, in_=accs[(pr, a, h)][:])
+            else:
+                nc.scalar.copy(out=dst, in_=accs[(pr, a, h)][:])
+
+        def drains_and_store(pr):
+            on_v = ((0, 1), (1, 1)) if pr % 2 == 1 else ((1, 1),)
+            for a in range(2):
+                for h in range(2):
+                    drain(pr, a, h, (a, h) in on_v)
+                if pr == 15:
+                    j = 2 + a
+                    nc.sync.dma_start(out=o_view[7][:, j:j + 1, :], in_=sts[pr][:, a:a + 1, :])
+            if pr != 15:
+                j = 2 * (pr % 2)
+                nc.sync.dma_start(out=o_view[pr // 2][:, j:j + 2, :], in_=sts[pr][:])
+
+        def multiply(pr):
+            for a in range(2):
+                for h in range(2):
+                    for c in range(2):
+                        mx_pass(pr, a, h, c)
+
+        def w_regroup(c, h):
+            for eng, lo, hi in ((nc.vector.tensor_copy, 0, V_COLS), (nc.scalar.copy, V_COLS, 512)):
+                eng(
+                    out=w_grp[c][h][:, lo:hi, :].rearrange("p (x i) t -> p x t i", i=4),
+                    in_=w_raw[c][:, :, 512 * h + lo:512 * h + hi].rearrange("p t (x i) -> p x t i", i=4),
+                )
+
+        def w_quantise(c, h):
+            nc.vector.quantize_mx(
+                out=w_codes[:, c, 512 * h:512 * (h + 1)].bitcast(E4),
+                scales=w_scales[:, c, 512 * h:512 * (h + 1)],
+                in_=w_grp[c][h][:].rearrange("p n t -> p (n t)"),
+            )
+
+        transposes(0)
+        copies(0)
+        quantise(0)
+        w_regroup(0, 0)
+        w_regroup(0, 1)
+        w_quantise(0, 0)
+        w_quantise(0, 1)
+        for h in range(2):
+            for a in range(2):
+                mx_pass(0, a, h, 0)
+        transposes(1)
+        w_regroup(1, 0)
+        w_regroup(1, 1)
+        w_quantise(1, 0)
+        w_quantise(1, 1)
+        for h in range(2):
+            for a in range(2):
+                mx_pass(0, a, h, 1)
+        copies(1)
+        quantise(1)
+        drains_and_store(0)
+        for k in range(1, 8):
+            transposes(2 * k)
+            transposes(2 * k + 1)
+            copies(2 * k)
+            copies(2 * k + 1)
+            quantise(2 * k)
+            quantise(2 * k + 1)
+            multiply(2 * k - 1)
+            drains_and_store(2 * k - 1)
+            multiply(2 * k)
+            drains_and_store(2 * k)
+        multiply(15)
+        drains_and_store(15)

@@ -17,7 +17,7 @@ N = 1024
 FLOPS = 2 * B * C * N
 BYTES = B * C * 2 + C * N * 2 + B * N * 4
 PINNED = True
-V_COLS = 336
+V_COLS = 272
 
 
 def tile_groupfc_t_kernel(tc, data, W, b, grad_out, out):
@@ -72,7 +72,7 @@ def tile_groupfc_t_kernel(tc, data, W, b, grad_out, out):
             for a in range(2):
                 dst = ggw[:, a, :].rearrange("p (c r u) -> p c r u", c=2, u=2)
                 src = xts[(pr, a)][:].rearrange("p (c u) r -> p c r u", u=2)
-                if a == 0:
+                if a == 0 and pr > 0:
                     nc.vector.tensor_copy(out=dst, in_=src)
                 else:
                     nc.scalar.copy(out=dst, in_=src)
@@ -109,14 +109,18 @@ def tile_groupfc_t_kernel(tc, data, W, b, grad_out, out):
 
         def drains_and_store(pr):
             on_v = ((0, 1), (1, 1)) if pr % 2 == 1 else ((1, 1),)
+            j = 2 * (pr % 2)
             for a in range(2):
                 for h in range(2):
                     drain(pr, a, h, (a, h) in on_v)
-                if pr == 15:
-                    j = 2 + a
-                    nc.sync.dma_start(out=o_view[7][:, j:j + 1, :], in_=sts[pr][:, a:a + 1, :])
-            if pr != 15:
-                j = 2 * (pr % 2)
+                    if pr == 15:
+                        nc.sync.dma_start(
+                            out=o_view[pr // 2][:, j + a:j + a + 1, 512 * h:512 * (h + 1)],
+                            in_=sts[pr][:, a:a + 1, 512 * h:512 * (h + 1)],
+                        )
+                if 12 <= pr < 15:
+                    nc.sync.dma_start(out=o_view[pr // 2][:, j + a:j + a + 1, :], in_=sts[pr][:, a:a + 1, :])
+            if pr < 12:
                 nc.sync.dma_start(out=o_view[pr // 2][:, j:j + 2, :], in_=sts[pr][:])
 
         def multiply(pr):
@@ -143,16 +147,16 @@ def tile_groupfc_t_kernel(tc, data, W, b, grad_out, out):
         copies(0)
         quantise(0)
         w_regroup(0, 0)
-        w_regroup(0, 1)
         w_quantise(0, 0)
+        w_regroup(0, 1)
         w_quantise(0, 1)
         for h in range(2):
             for a in range(2):
                 mx_pass(0, a, h, 0)
         transposes(1)
         w_regroup(1, 0)
-        w_regroup(1, 1)
         w_quantise(1, 0)
+        w_regroup(1, 1)
         w_quantise(1, 1)
         for h in range(2):
             for a in range(2):

@@ -17,7 +17,7 @@ N = 1024
 FLOPS = 2 * B * C * N
 BYTES = B * C * 2 + C * N * 2 + B * N * 4
 PINNED = True
-V_COLS = 272
+V_COLS = 336
 
 
 def tile_groupfc_t_kernel(tc, data, W, b, grad_out, out):
@@ -27,15 +27,15 @@ def tile_groupfc_t_kernel(tc, data, W, b, grad_out, out):
             ctx.enter_context(tc.manual_schedule())
         keep = ctx.enter_context(tc.tile_pool(name="keep", bufs=1))
         grp = ctx.enter_context(tc.tile_pool(name="grp", bufs=3))
-        stg = ctx.enter_context(tc.tile_pool(name="stg", bufs=10))
+        stg = ctx.enter_context(tc.tile_pool(name="stg", bufs=5))
         ps = ctx.enter_context(tc.psum_pool(name="ps", bufs=4))
 
         ident = keep.tile([P, P], F32, name="ident")
         masks.make_identity(nc, ident[:])
 
-        g_view = [grad_out[512 * m:512 * (m + 1), :].rearrange("(p j) c -> p j c", j=4) for m in range(8)]
-        o_view = [out[512 * m:512 * (m + 1), :].rearrange("(p j) n -> p j n", j=4) for m in range(8)]
-        g_sb = [keep.tile([P, 4, C], BF16, name="g%d" % m) for m in range(8)]
+        g_view = [grad_out[1024 * m:1024 * (m + 1), :].rearrange("(p j) c -> p j c", j=8) for m in range(4)]
+        o_view = [out[1024 * m:1024 * (m + 1), :].rearrange("(p j) n -> p j n", j=8) for m in range(4)]
+        g_sb = [keep.tile([P, 8, C], BF16, name="g%d" % m) for m in range(4)]
         w_raw = [keep.tile([P, 4, N], BF16, name="wr%d" % c) for c in range(2)]
         w_grp = [[keep.tile([P, 512, 4], BF16, name="wg%d%d" % (c, h), align_bytes=64) for h in range(2)] for c in range(2)]
         w_codes = keep.tile([P, 2, N], U32, name="w_codes", align_bytes=64)
@@ -48,7 +48,8 @@ def tile_groupfc_t_kernel(tc, data, W, b, grad_out, out):
                 in_=W[512 * c:512 * (c + 1), :].rearrange("(u q e) n -> q u (e n)", u=2, e=2),
             )
         nc.sync.dma_start(out=g_sb[0][:, 2:4, :], in_=g_view[0][:, 2:4, :])
-        for m in range(1, 8):
+        nc.sync.dma_start(out=g_sb[0][:, 4:8, :], in_=g_view[0][:, 4:8, :])
+        for m in range(1, 4):
             nc.sync.dma_start(out=g_sb[m][:], in_=g_view[m])
 
         xts = {}
@@ -58,12 +59,12 @@ def tile_groupfc_t_kernel(tc, data, W, b, grad_out, out):
         sts = {}
 
         def transposes(pr):
-            words = g_sb[pr // 2][:].bitcast(F32)
+            words = g_sb[pr // 4][:].bitcast(F32)
             for a in range(2):
                 xt = ps.tile([P, 4, P], F32, name="xt", tag="xt")
                 xts[(pr, a)] = xt
                 for s in range(4):
-                    nc.tensor.transpose(xt[:, s, :], words[:, 2 * (pr % 2) + a, P * s:P * (s + 1)], ident[:])
+                    nc.tensor.transpose(xt[:, s, :], words[:, 2 * (pr % 4) + a, P * s:P * (s + 1)], ident[:])
 
         def copies(pr):
             gg = grp.tile([P, 2, C], BF16, name="gg", tag="gg", align_bytes=64)
@@ -72,7 +73,7 @@ def tile_groupfc_t_kernel(tc, data, W, b, grad_out, out):
             for a in range(2):
                 dst = ggw[:, a, :].rearrange("p (c r u) -> p c r u", c=2, u=2)
                 src = xts[(pr, a)][:].rearrange("p (c u) r -> p c r u", u=2)
-                if a == 0 and pr > 0:
+                if a == 0:
                     nc.vector.tensor_copy(out=dst, in_=src)
                 else:
                     nc.scalar.copy(out=dst, in_=src)
@@ -99,9 +100,9 @@ def tile_groupfc_t_kernel(tc, data, W, b, grad_out, out):
             )
 
         def drain(pr, a, h, on_vector):
-            if (a, h) == (0, 0):
-                sts[pr] = stg.tile([P, 2, N], F32, name="st", tag="st")
-            dst = sts[pr][:, a, 512 * h:512 * (h + 1)]
+            if (pr % 2, a, h) == (0, 0, 0):
+                sts[pr // 2] = stg.tile([P, 4, N], F32, name="st", tag="st")
+            dst = sts[pr // 2][:, 2 * (pr % 2) + a, 512 * h:512 * (h + 1)]
             if on_vector:
                 nc.vector.tensor_copy(out=dst, in_=accs[(pr, a, h)][:])
             else:
@@ -109,19 +110,17 @@ def tile_groupfc_t_kernel(tc, data, W, b, grad_out, out):
 
         def drains_and_store(pr):
             on_v = ((0, 1), (1, 1)) if pr % 2 == 1 else ((1, 1),)
-            j = 2 * (pr % 2)
             for a in range(2):
                 for h in range(2):
                     drain(pr, a, h, (a, h) in on_v)
-                    if pr == 15:
-                        nc.sync.dma_start(
-                            out=o_view[pr // 2][:, j + a:j + a + 1, 512 * h:512 * (h + 1)],
-                            in_=sts[pr][:, a:a + 1, 512 * h:512 * (h + 1)],
-                        )
-                if 12 <= pr < 15:
-                    nc.sync.dma_start(out=o_view[pr // 2][:, j + a:j + a + 1, :], in_=sts[pr][:, a:a + 1, :])
-            if pr < 12:
-                nc.sync.dma_start(out=o_view[pr // 2][:, j:j + 2, :], in_=sts[pr][:])
+                if pr == 15:
+                    nc.sync.dma_start(out=o_view[3][:, 6 + a:7 + a, :], in_=sts[7][:, 2 + a:3 + a, :])
+            j = 2 * (pr % 4)
+            if pr < 8 and pr % 2 == 1:
+                nc.sync.dma_start(out=o_view[pr // 4][:, j - 2:j + 2, :], in_=sts[pr // 2][:])
+            if 8 <= pr < 15:
+                s0 = 2 * (pr % 2)
+                nc.sync.dma_start(out=o_view[pr // 4][:, j:j + 2, :], in_=sts[pr // 2][:, s0:s0 + 2, :])
 
         def multiply(pr):
             for a in range(2):
@@ -147,16 +146,16 @@ def tile_groupfc_t_kernel(tc, data, W, b, grad_out, out):
         copies(0)
         quantise(0)
         w_regroup(0, 0)
-        w_quantise(0, 0)
         w_regroup(0, 1)
+        w_quantise(0, 0)
         w_quantise(0, 1)
         for h in range(2):
             for a in range(2):
                 mx_pass(0, a, h, 0)
         transposes(1)
         w_regroup(1, 0)
-        w_quantise(1, 0)
         w_regroup(1, 1)
+        w_quantise(1, 0)
         w_quantise(1, 1)
         for h in range(2):
             for a in range(2):

@@ -18,6 +18,7 @@ FLOPS = 2 * B * C * N
 BYTES = B * C * 2 + C * N * 2 + B * N * 4
 PINNED = True
 V_COLS = 336
+BUNCHES = (2, 3, 3, 3, 3)
 
 
 def tile_groupfc_t_kernel(tc, data, W, b, grad_out, out):
@@ -26,16 +27,23 @@ def tile_groupfc_t_kernel(tc, data, W, b, grad_out, out):
         if PINNED:
             ctx.enter_context(tc.manual_schedule())
         keep = ctx.enter_context(tc.tile_pool(name="keep", bufs=1))
-        grp = ctx.enter_context(tc.tile_pool(name="grp", bufs=3))
-        stg = ctx.enter_context(tc.tile_pool(name="stg", bufs=5))
-        ps = ctx.enter_context(tc.psum_pool(name="ps", bufs=4))
+        grp = ctx.enter_context(tc.tile_pool(name="grp", bufs=5))
+        stg = ctx.enter_context(tc.tile_pool(name="stg", bufs=10))
+        ps = ctx.enter_context(tc.psum_pool(name="ps", bufs=1))
+        banks_used = [0]
+
+        def next_bank(shape):
+            tag = "bank%d" % (banks_used[0] % 8)
+            banks_used[0] += 1
+            return ps.tile(shape, F32, name=tag, tag=tag)
+
 
         ident = keep.tile([P, P], F32, name="ident")
         masks.make_identity(nc, ident[:])
 
-        g_view = [grad_out[1024 * m:1024 * (m + 1), :].rearrange("(p j) c -> p j c", j=8) for m in range(4)]
-        o_view = [out[1024 * m:1024 * (m + 1), :].rearrange("(p j) n -> p j n", j=8) for m in range(4)]
-        g_sb = [keep.tile([P, 8, C], BF16, name="g%d" % m) for m in range(4)]
+        g_view = [grad_out[512 * m:512 * (m + 1), :].rearrange("(p j) c -> p j c", j=4) for m in range(8)]
+        o_view = [out[512 * m:512 * (m + 1), :].rearrange("(p j) n -> p j n", j=4) for m in range(8)]
+        g_sb = [keep.tile([P, 4, C], BF16, name="g%d" % m) for m in range(8)]
         w_raw = [keep.tile([P, 4, N], BF16, name="wr%d" % c) for c in range(2)]
         w_grp = [[keep.tile([P, 512, 4], BF16, name="wg%d%d" % (c, h), align_bytes=64) for h in range(2)] for c in range(2)]
         w_codes = keep.tile([P, 2, N], U32, name="w_codes", align_bytes=64)
@@ -48,8 +56,7 @@ def tile_groupfc_t_kernel(tc, data, W, b, grad_out, out):
                 in_=W[512 * c:512 * (c + 1), :].rearrange("(u q e) n -> q u (e n)", u=2, e=2),
             )
         nc.sync.dma_start(out=g_sb[0][:, 2:4, :], in_=g_view[0][:, 2:4, :])
-        nc.sync.dma_start(out=g_sb[0][:, 4:8, :], in_=g_view[0][:, 4:8, :])
-        for m in range(1, 4):
+        for m in range(1, 8):
             nc.sync.dma_start(out=g_sb[m][:], in_=g_view[m])
 
         xts = {}
@@ -59,12 +66,12 @@ def tile_groupfc_t_kernel(tc, data, W, b, grad_out, out):
         sts = {}
 
         def transposes(pr):
-            words = g_sb[pr // 4][:].bitcast(F32)
+            words = g_sb[pr // 2][:].bitcast(F32)
             for a in range(2):
-                xt = ps.tile([P, 4, P], F32, name="xt", tag="xt")
+                xt = next_bank([P, 4, P])
                 xts[(pr, a)] = xt
                 for s in range(4):
-                    nc.tensor.transpose(xt[:, s, :], words[:, 2 * (pr % 4) + a, P * s:P * (s + 1)], ident[:])
+                    nc.tensor.transpose(xt[:, s, :], words[:, 2 * (pr % 2) + a, P * s:P * (s + 1)], ident[:])
 
         def copies(pr):
             gg = grp.tile([P, 2, C], BF16, name="gg", tag="gg", align_bytes=64)
@@ -86,7 +93,7 @@ def tile_groupfc_t_kernel(tc, data, W, b, grad_out, out):
 
         def mx_pass(pr, a, h, c):
             if c == 0:
-                accs[(pr, a, h)] = ps.tile([P, 512], F32, name="acc", tag="acc")
+                accs[(pr, a, h)] = next_bank([P, 512])
             gc, gs = gcs[pr]
             lo = 256 * a + P * c
             nc.tensor.matmul_mx(
@@ -100,9 +107,9 @@ def tile_groupfc_t_kernel(tc, data, W, b, grad_out, out):
             )
 
         def drain(pr, a, h, on_vector):
-            if (pr % 2, a, h) == (0, 0, 0):
-                sts[pr // 2] = stg.tile([P, 4, N], F32, name="st", tag="st")
-            dst = sts[pr // 2][:, 2 * (pr % 2) + a, 512 * h:512 * (h + 1)]
+            if (a, h) == (0, 0):
+                sts[pr] = stg.tile([P, 2, N], F32, name="st", tag="st")
+            dst = sts[pr][:, a, 512 * h:512 * (h + 1)]
             if on_vector:
                 nc.vector.tensor_copy(out=dst, in_=accs[(pr, a, h)][:])
             else:
@@ -113,14 +120,15 @@ def tile_groupfc_t_kernel(tc, data, W, b, grad_out, out):
             for a in range(2):
                 for h in range(2):
                     drain(pr, a, h, (a, h) in on_v)
-                if pr == 15:
-                    nc.sync.dma_start(out=o_view[3][:, 6 + a:7 + a, :], in_=sts[7][:, 2 + a:3 + a, :])
-            j = 2 * (pr % 4)
-            if pr < 8 and pr % 2 == 1:
-                nc.sync.dma_start(out=o_view[pr // 4][:, j - 2:j + 2, :], in_=sts[pr // 2][:])
-            if 8 <= pr < 15:
-                s0 = 2 * (pr % 2)
-                nc.sync.dma_start(out=o_view[pr // 4][:, j:j + 2, :], in_=sts[pr // 2][:, s0:s0 + 2, :])
+                    if pr == 15 and a == 1:
+                        nc.sync.dma_start(
+                            out=o_view[7][:, 3:4, 512 * h:512 * (h + 1)], in_=sts[pr][:, 1:2, 512 * h:512 * (h + 1)]
+                        )
+                if pr == 15 and a == 0:
+                    nc.sync.dma_start(out=o_view[7][:, 2:3, :], in_=sts[pr][:, 0:1, :])
+            if pr != 15:
+                j = 2 * (pr % 2)
+                nc.sync.dma_start(out=o_view[pr // 2][:, j:j + 2, :], in_=sts[pr][:])
 
         def multiply(pr):
             for a in range(2):
@@ -149,10 +157,13 @@ def tile_groupfc_t_kernel(tc, data, W, b, grad_out, out):
         w_regroup(0, 1)
         w_quantise(0, 0)
         w_quantise(0, 1)
+        banks_used[0] = 4
         for h in range(2):
             for a in range(2):
                 mx_pass(0, a, h, 0)
+        banks_used[0] = 2
         transposes(1)
+        banks_used[0] = 8
         w_regroup(1, 0)
         w_regroup(1, 1)
         w_quantise(1, 0)
@@ -163,16 +174,18 @@ def tile_groupfc_t_kernel(tc, data, W, b, grad_out, out):
         copies(1)
         quantise(1)
         drains_and_store(0)
-        for k in range(1, 8):
-            transposes(2 * k)
-            transposes(2 * k + 1)
-            copies(2 * k)
-            copies(2 * k + 1)
-            quantise(2 * k)
-            quantise(2 * k + 1)
-            multiply(2 * k - 1)
-            drains_and_store(2 * k - 1)
-            multiply(2 * k)
-            drains_and_store(2 * k)
+        first = 2
+        for size in BUNCHES:
+            prs = list(range(first, first + size))
+            for pr in prs:
+                transposes(pr)
+            for pr in prs:
+                copies(pr)
+            for pr in prs:
+                quantise(pr)
+            for pr in prs:
+                multiply(pr - 1)
+                drains_and_store(pr - 1)
+            first += size
         multiply(15)
         drains_and_store(15)

@@ -17,7 +17,7 @@ N = 1024
 FLOPS = 2 * B * C * N
 BYTES = B * C * 2 + C * N * 2 + B * N * 4
 PINNED = True
-V_COLS = 336
+V_COLS = 256
 BUNCHES = (2, 3, 3, 3, 3)
 
 
@@ -37,6 +37,14 @@ def tile_groupfc_t_kernel(tc, data, W, b, grad_out, out):
             banks_used[0] += 1
             return ps.tile(shape, F32, name=tag, tag=tag)
 
+
+        warm = keep.tile([P, 512], BF16, name="warm")
+        nc.vector.memset(warm[:], 0.0)
+        warm_out = ps.tile([P, 512], F32, name="bank7", tag="bank7")
+
+        def warm_up(count):
+            for i in range(count):
+                nc.tensor.matmul(warm_out[:], lhsT=warm[:, 0:P], rhs=warm[:], start=True, stop=True)
 
         ident = keep.tile([P, P], F32, name="ident")
         masks.make_identity(nc, ident[:])
@@ -73,14 +81,14 @@ def tile_groupfc_t_kernel(tc, data, W, b, grad_out, out):
                 for s in range(4):
                     nc.tensor.transpose(xt[:, s, :], words[:, 2 * (pr % 2) + a, P * s:P * (s + 1)], ident[:])
 
-        def copies(pr):
+        def copies(pr, engs="VS"):
             gg = grp.tile([P, 2, C], BF16, name="gg", tag="gg", align_bytes=64)
             ggs[pr] = gg
             ggw = gg[:].bitcast(F32)
             for a in range(2):
                 dst = ggw[:, a, :].rearrange("p (c r u) -> p c r u", c=2, u=2)
                 src = xts[(pr, a)][:].rearrange("p (c u) r -> p c r u", u=2)
-                if a == 0:
+                if engs[a] == "V":
                     nc.vector.tensor_copy(out=dst, in_=src)
                 else:
                     nc.scalar.copy(out=dst, in_=src)
@@ -150,10 +158,12 @@ def tile_groupfc_t_kernel(tc, data, W, b, grad_out, out):
                 in_=w_grp[c][h][:].rearrange("p n t -> p (n t)"),
             )
 
+        warm_up(8)
         transposes(0)
+        warm_up(8)
         copies(0)
-        quantise(0)
         w_regroup(0, 0)
+        quantise(0)
         w_regroup(0, 1)
         w_quantise(0, 0)
         w_quantise(0, 1)
@@ -171,7 +181,7 @@ def tile_groupfc_t_kernel(tc, data, W, b, grad_out, out):
         for h in range(2):
             for a in range(2):
                 mx_pass(0, a, h, 1)
-        copies(1)
+        copies(1, "SS")
         quantise(1)
         drains_and_store(0)
         first = 2

@@ -125,17 +125,18 @@ def tile_groupfc_t_kernel(tc, data, W, b, grad_out, out):
 
         def drains_and_store(pr):
             on_v = ((0, 1), (1, 1)) if pr % 2 == 1 else ((1, 1),)
+            j = 2 * (pr % 2)
             for a in range(2):
                 for h in range(2):
                     drain(pr, a, h, (a, h) in on_v)
-                    if pr == 15 and a == 1:
+                    if 2 * pr + a >= 31:
                         nc.sync.dma_start(
-                            out=o_view[7][:, 3:4, 512 * h:512 * (h + 1)], in_=sts[pr][:, 1:2, 512 * h:512 * (h + 1)]
+                            out=o_view[pr // 2][:, j + a:j + a + 1, 512 * h:512 * (h + 1)],
+                            in_=sts[pr][:, a:a + 1, 512 * h:512 * (h + 1)],
                         )
-                if pr == 15 and a == 0:
-                    nc.sync.dma_start(out=o_view[7][:, 2:3, :], in_=sts[pr][:, 0:1, :])
-            if pr != 15:
-                j = 2 * (pr % 2)
+                if pr >= 12 and 2 * pr + a < 31:
+                    nc.sync.dma_start(out=o_view[pr // 2][:, j + a:j + a + 1, :], in_=sts[pr][:, a:a + 1, :])
+            if pr < 12:
                 nc.sync.dma_start(out=o_view[pr // 2][:, j:j + 2, :], in_=sts[pr][:])
 
         def multiply(pr):

@@ -54,7 +54,12 @@ def tile_groupfc_t_kernel(tc, data, W, b, grad_out, out):
         g_sb = [keep.tile([P, 4, C], BF16, name="g%d" % m) for m in range(8)]
         w_raw = [keep.tile([P, 4, N], BF16, name="wr%d" % c) for c in range(2)]
         w_grp = [[keep.tile([P, 512, 4], BF16, name="wg%d%d" % (c, h), align_bytes=64) for h in range(2)] for c in range(2)]
-        w_codes = keep.tile([P, 2, N], U32, name="w_codes", align_bytes=64)
+        w_codes = keep.tile([P, 4, 512 + 64], U32, name="w_codes", align_bytes=256)
+
+        def w_words(c, h):
+            k = 2 * c + h
+            return w_codes[:, k, 16 * k:16 * k + 512]
+
         w_scales = keep.tile([P, 2, N], U8, name="w_scales", align_bytes=64)
 
         nc.sync.dma_start(out=g_sb[0][:, 0:2, :], in_=g_view[0][:, 0:2, :])
@@ -108,7 +113,7 @@ def tile_groupfc_t_kernel(tc, data, W, b, grad_out, out):
                 out=accs[(pr, a, h)][:],
                 lhsT=gc[:, lo:lo + P].bitcast(E5),
                 lhsT_scale=gs[:, lo:lo + P],
-                rhs=w_codes[:, c, 512 * h:512 * (h + 1)].bitcast(E4),
+                rhs=w_words(c, h).bitcast(E4),
                 rhs_scale=w_scales[:, c, 512 * h:512 * (h + 1)],
                 start=(c == 0),
                 stop=(c == 1),
@@ -154,7 +159,7 @@ def tile_groupfc_t_kernel(tc, data, W, b, grad_out, out):
 
         def w_quantise(c, h):
             nc.vector.quantize_mx(
-                out=w_codes[:, c, 512 * h:512 * (h + 1)].bitcast(E4),
+                out=w_words(c, h).bitcast(E4),
                 scales=w_scales[:, c, 512 * h:512 * (h + 1)],
                 in_=w_grp[c][h][:].rearrange("p n t -> p (n t)"),
             )

@@ -19,6 +19,8 @@ BYTES = B * C * 2 + C * N * 2 + B * N * 4
 PINNED = True
 V_COLS = 256
 BUNCHES = (2, 3, 3, 3, 3)
+G_LOADS = ((0,), (1,), (2, 3), (4, 5, 6, 7))
+MERGED = 8
 
 
 def tile_groupfc_t_kernel(tc, data, W, b, grad_out, out):
@@ -51,7 +53,11 @@ def tile_groupfc_t_kernel(tc, data, W, b, grad_out, out):
 
         g_view = [grad_out[512 * m:512 * (m + 1), :].rearrange("(p j) c -> p j c", j=4) for m in range(8)]
         o_view = [out[512 * m:512 * (m + 1), :].rearrange("(p j) n -> p j n", j=4) for m in range(8)]
-        g_sb = [keep.tile([P, 4, C], BF16, name="g%d" % m) for m in range(8)]
+        g_big = [keep.tile([P, len(blocks), 4, C], BF16, name="g%d" % blocks[0]) for blocks in G_LOADS]
+        g_sb = {}
+        for tile_, blocks in zip(g_big, G_LOADS):
+            for i, m in enumerate(blocks):
+                g_sb[m] = tile_[:, i, :, :]
         w_raw = [keep.tile([P, 4, N], BF16, name="wr%d" % c) for c in range(2)]
         w_grp = [[keep.tile([P, 512, 4], BF16, name="wg%d%d" % (c, h), align_bytes=64) for h in range(2)] for c in range(2)]
         w_codes = keep.tile([P, 4, 512 + 64], U32, name="w_codes", align_bytes=256)
@@ -69,8 +75,12 @@ def tile_groupfc_t_kernel(tc, data, W, b, grad_out, out):
                 in_=W[512 * c:512 * (c + 1), :].rearrange("(u q e) n -> q u (e n)", u=2, e=2),
             )
         nc.sync.dma_start(out=g_sb[0][:, 2:4, :], in_=g_view[0][:, 2:4, :])
-        for m in range(1, 8):
-            nc.sync.dma_start(out=g_sb[m][:], in_=g_view[m])
+        for tile_, blocks in zip(g_big[1:], G_LOADS[1:]):
+            lo = 512 * blocks[0]
+            nc.sync.dma_start(
+                out=tile_[:].rearrange("p b j c -> p b (j c)"),
+                in_=grad_out[lo:lo + 512 * len(blocks), :].rearrange("(b p j) c -> p b (j c)", b=len(blocks), j=4),
+            )
 
         xts = {}
         ggs = {}
@@ -79,7 +89,7 @@ def tile_groupfc_t_kernel(tc, data, W, b, grad_out, out):
         sts = {}
 
         def transposes(pr):
-            words = g_sb[pr // 2][:].bitcast(F32)
+            words = g_sb[pr // 2].bitcast(F32)
             for a in range(2):
                 xt = next_bank([P, 4, P])
                 xts[(pr, a)] = xt
@@ -120,9 +130,13 @@ def tile_groupfc_t_kernel(tc, data, W, b, grad_out, out):
             )
 
         def drain(pr, a, h, on_vector):
-            if (a, h) == (0, 0):
-                sts[pr] = stg.tile([P, 2, N], F32, name="st", tag="st")
-            dst = sts[pr][:, a, 512 * h:512 * (h + 1)]
+            head = pr - pr % 2 if pr < MERGED else pr
+            if head not in sts:
+                if pr < MERGED:
+                    sts[head] = stg.tile([P, 4, N], F32, name="st4", tag="st4", bufs=3)
+                else:
+                    sts[head] = stg.tile([P, 2, N], F32, name="st2", tag="st2", bufs=4)
+            dst = sts[head][:, 2 * (pr - head) + a, 512 * h:512 * (h + 1)]
             if on_vector:
                 nc.vector.tensor_copy(out=dst, in_=accs[(pr, a, h)][:])
             else:
@@ -141,7 +155,10 @@ def tile_groupfc_t_kernel(tc, data, W, b, grad_out, out):
                         )
                 if pr >= 12 and 2 * pr + a < 31:
                     nc.sync.dma_start(out=o_view[pr // 2][:, j + a:j + a + 1, :], in_=sts[pr][:, a:a + 1, :])
-            if pr < 12:
+            if pr < MERGED:
+                if pr % 2 == 1:
+                    nc.sync.dma_start(out=o_view[pr // 2], in_=sts[pr - 1][:])
+            elif pr < 12:
                 nc.sync.dma_start(out=o_view[pr // 2][:, j:j + 2, :], in_=sts[pr][:])
 
         def multiply(pr):

@@ -40,14 +40,6 @@ def tile_groupfc_t_kernel(tc, data, W, b, grad_out, out):
             return ps.tile(shape, F32, name=tag, tag=tag)
 
 
-        warm = keep.tile([P, 512], BF16, name="warm")
-        nc.vector.memset(warm[:], 0.0)
-        warm_out = ps.tile([P, 512], F32, name="bank7", tag="bank7")
-
-        def warm_up(count):
-            for i in range(count):
-                nc.tensor.matmul(warm_out[:], lhsT=warm[:, 0:P], rhs=warm[:], start=True, stop=True)
-
         ident = keep.tile([P, P], F32, name="ident")
         masks.make_identity(nc, ident[:])
 
@@ -60,12 +52,7 @@ def tile_groupfc_t_kernel(tc, data, W, b, grad_out, out):
                 g_sb[m] = tile_[:, i, :, :]
         w_raw = [keep.tile([P, 4, N], BF16, name="wr%d" % c) for c in range(2)]
         w_grp = [[keep.tile([P, 512, 4], BF16, name="wg%d%d" % (c, h), align_bytes=64) for h in range(2)] for c in range(2)]
-        w_codes = keep.tile([P, 4, 512 + 64], U32, name="w_codes", align_bytes=256)
-
-        def w_words(c, h):
-            k = 2 * c + h
-            return w_codes[:, k, 16 * k:16 * k + 512]
-
+        w_codes = keep.tile([P, 2, N], U32, name="w_codes", align_bytes=64)
         w_scales = keep.tile([P, 2, N], U8, name="w_scales", align_bytes=64)
 
         nc.sync.dma_start(out=g_sb[0][:, 0:2, :], in_=g_view[0][:, 0:2, :])
@@ -123,7 +110,7 @@ def tile_groupfc_t_kernel(tc, data, W, b, grad_out, out):
                 out=accs[(pr, a, h)][:],
                 lhsT=gc[:, lo:lo + P].bitcast(E5),
                 lhsT_scale=gs[:, lo:lo + P],
-                rhs=w_words(c, h).bitcast(E4),
+                rhs=w_codes[:, c, 512 * h:512 * (h + 1)].bitcast(E4),
                 rhs_scale=w_scales[:, c, 512 * h:512 * (h + 1)],
                 start=(c == 0),
                 stop=(c == 1),
@@ -176,14 +163,12 @@ def tile_groupfc_t_kernel(tc, data, W, b, grad_out, out):
 
         def w_quantise(c, h):
             nc.vector.quantize_mx(
-                out=w_words(c, h).bitcast(E4),
+                out=w_codes[:, c, 512 * h:512 * (h + 1)].bitcast(E4),
                 scales=w_scales[:, c, 512 * h:512 * (h + 1)],
                 in_=w_grp[c][h][:].rearrange("p n t -> p (n t)"),
             )
 
-        warm_up(8)
         transposes(0)
-        warm_up(8)
         copies(0)
         w_regroup(0, 0)
         quantise(0)

from contextlib import ExitStack

import concourse.masks as masks
import concourse.mybir as mybir

F32 = mybir.dt.float32
BF16 = mybir.dt.bfloat16
U32 = mybir.dt.uint32
U8 = mybir.dt.uint8
E4 = mybir.dt.float8_e4m3fn_x4
E5 = mybir.dt.float8_e5m2_x4

P = 128
B = 4096
C = 1024
N = 1024
FLOPS = 2 * B * C * N
BYTES = B * C * 2 + C * N * 2 + B * N * 4
PINNED = True
V_COLS = 256
BUNCHES = (2, 3, 3, 3, 3)
G_LOADS = ((0,), (1,), (2, 3), (4, 5, 6, 7))
MERGED = 8


def tile_groupfc_t_kernel(tc, data, W, b, grad_out, out):
    nc = tc.nc
    with ExitStack() as ctx:
        if PINNED:
            ctx.enter_context(tc.manual_schedule())
        keep = ctx.enter_context(tc.tile_pool(name="keep", bufs=1))
        grp = ctx.enter_context(tc.tile_pool(name="grp", bufs=5))
        stg = ctx.enter_context(tc.tile_pool(name="stg", bufs=10))
        ps = ctx.enter_context(tc.psum_pool(name="ps", bufs=1))
        banks_used = [0]

        def next_bank(shape):
            tag = "bank%d" % (banks_used[0] % 8)
            banks_used[0] += 1
            return ps.tile(shape, F32, name=tag, tag=tag)


        ident = keep.tile([P, P], F32, name="ident")
        masks.make_identity(nc, ident[:])

        g_view = [grad_out[512 * m:512 * (m + 1), :].rearrange("(p j) c -> p j c", j=4) for m in range(8)]
        o_view = [out[512 * m:512 * (m + 1), :].rearrange("(p j) n -> p j n", j=4) for m in range(8)]
        g_big = [keep.tile([P, len(blocks), 4, C], BF16, name="g%d" % blocks[0]) for blocks in G_LOADS]
        g_sb = {}
        for tile_, blocks in zip(g_big, G_LOADS):
            for i, m in enumerate(blocks):
                g_sb[m] = tile_[:, i, :, :]
        w_raw = [keep.tile([P, 4, N], BF16, name="wr%d" % c) for c in range(2)]
        w_grp = [[keep.tile([P, 512, 4], BF16, name="wg%d%d" % (c, h), align_bytes=64) for h in range(2)] for c in range(2)]
        w_codes = keep.tile([P, 2, N], U32, name="w_codes", align_bytes=64)
        w_scales = keep.tile([P, 2, N], U8, name="w_scales", align_bytes=64)

        nc.sync.dma_start(out=g_sb[0][:, 0:2, :], in_=g_view[0][:, 0:2, :])
        for c in range(2):
            nc.sync.dma_start(
                out=w_raw[c][:].rearrange("p (u e) n -> p u (e n)", u=2),
                in_=W[512 * c:512 * (c + 1), :].rearrange("(u q e) n -> q u (e n)", u=2, e=2),
            )
        nc.sync.dma_start(out=g_sb[0][:, 2:4, :], in_=g_view[0][:, 2:4, :])
        for tile_, blocks in zip(g_big[1:], G_LOADS[1:]):
            lo = 512 * blocks[0]
            nc.sync.dma_start(
                out=tile_[:].rearrange("p b j c -> p b (j c)"),
                in_=grad_out[lo:lo + 512 * len(blocks), :].rearrange("(b p j) c -> p b (j c)", b=len(blocks), j=4),
            )

        xts = {}
        ggs = {}
        gcs = {}
        accs = {}
        sts = {}

        def transposes(pr):
            words = g_sb[pr // 2].bitcast(F32)
            for a in range(2):
                xt = next_bank([P, 4, P])
                xts[(pr, a)] = xt
                for s in range(4):
                    nc.tensor.transpose(xt[:, s, :], words[:, 2 * (pr % 2) + a, P * s:P * (s + 1)], ident[:])

        def copies(pr, engs="VS"):
            gg = grp.tile([P, 2, C], BF16, name="gg", tag="gg", align_bytes=64)
            ggs[pr] = gg
            ggw = gg[:].bitcast(F32)
            for a in range(2):
                dst = ggw[:, a, :].rearrange("p (c r u) -> p c r u", c=2, u=2)
                src = xts[(pr, a)][:].rearrange("p (c u) r -> p c r u", u=2)
                if engs[a] == "V":
                    nc.vector.tensor_copy(out=dst, in_=src)
                else:
                    nc.scalar.copy(out=dst, in_=src)

        def quantise(pr):
            gc = grp.tile([P, 512], U32, name="gc", tag="gc", align_bytes=64)
            gs = grp.tile([P, 512], U8, name="gs", tag="gs", align_bytes=64)
            gcs[pr] = (gc, gs)
            nc.vector.quantize_mx(out=gc[:].bitcast(E5), scales=gs[:], in_=ggs[pr][:].rearrange("p a k -> p (a k)"))

        def mx_pass(pr, a, h, c):
            if c == 0:
                accs[(pr, a, h)] = next_bank([P, 512])
            gc, gs = gcs[pr]
            lo = 256 * a + P * c
            nc.tensor.matmul_mx(
                out=accs[(pr, a, h)][:],
                lhsT=gc[:, lo:lo + P].bitcast(E5),
                lhsT_scale=gs[:, lo:lo + P],
                rhs=w_codes[:, c, 512 * h:512 * (h + 1)].bitcast(E4),
                rhs_scale=w_scales[:, c, 512 * h:512 * (h + 1)],
                start=(c == 0),
                stop=(c == 1),
            )

        def drain(pr, a, h, on_vector):
            head = pr - pr % 2 if pr < MERGED else pr
            if head not in sts:
                if pr < MERGED:
                    sts[head] = stg.tile([P, 4, N], F32, name="st4", tag="st4", bufs=3)
                else:
                    sts[head] = stg.tile([P, 2, N], F32, name="st2", tag="st2", bufs=4)
            dst = sts[head][:, 2 * (pr - head) + a, 512 * h:512 * (h + 1)]
            if on_vector:
                nc.vector.tensor_copy(out=dst, in_=accs[(pr, a, h)][:])
            else:
                nc.scalar.copy(out=dst, in_=accs[(pr, a, h)][:])

        def drains_and_store(pr):
            on_v = ((0, 1), (1, 1)) if pr % 2 == 1 else ((1, 1),)
            j = 2 * (pr % 2)
            for a in range(2):
                for h in range(2):
                    drain(pr, a, h, (a, h) in on_v)
                    if 2 * pr + a >= 31:
                        nc.sync.dma_start(
                            out=o_view[pr // 2][:, j + a:j + a + 1, 512 * h:512 * (h + 1)],
                            in_=sts[pr][:, a:a + 1, 512 * h:512 * (h + 1)],
                        )
                if pr >= 12 and 2 * pr + a < 31:
                    nc.sync.dma_start(out=o_view[pr // 2][:, j + a:j + a + 1, :], in_=sts[pr][:, a:a + 1, :])
            if pr < MERGED:
                if pr % 2 == 1:
                    nc.sync.dma_start(out=o_view[pr // 2], in_=sts[pr - 1][:])
            elif pr < 12:
                nc.sync.dma_start(out=o_view[pr // 2][:, j:j + 2, :], in_=sts[pr][:])

        def multiply(pr):
            for a in range(2):
                for h in range(2):
                    for c in range(2):
                        mx_pass(pr, a, h, c)

        def w_regroup(c, h):
            for eng, lo, hi in ((nc.vector.tensor_copy, 0, V_COLS), (nc.scalar.copy, V_COLS, 512)):
                eng(
                    out=w_grp[c][h][:, lo:hi, :].rearrange("p (x i) t -> p x t i", i=4),
                    in_=w_raw[c][:, :, 512 * h + lo:512 * h + hi].rearrange("p t (x i) -> p x t i", i=4),
                )

        def w_quantise(c, h):
            nc.vector.quantize_mx(
                out=w_codes[:, c, 512 * h:512 * (h + 1)].bitcast(E4),
                scales=w_scales[:, c, 512 * h:512 * (h + 1)],
                in_=w_grp[c][h][:].rearrange("p n t -> p (n t)"),
            )

        transposes(0)
        copies(0)
        w_regroup(0, 0)
        quantise(0)
        w_regroup(0, 1)
        w_quantise(0, 0)
        w_quantise(0, 1)
        banks_used[0] = 4
        for h in range(2):
            for a in range(2):
                mx_pass(0, a, h, 0)
        banks_used[0] = 2
        transposes(1)
        banks_used[0] = 8
        w_regroup(1, 0)
        w_regroup(1, 1)
        w_quantise(1, 0)
        w_quantise(1, 1)
        for h in range(2):
            for a in range(2):
                mx_pass(0, a, h, 1)
        copies(1, "SS")
        quantise(1)
        drains_and_store(0)
        first = 2
        for size in BUNCHES:
            prs = list(range(first, first + size))
            for pr in prs:
                transposes(pr)
            for pr in prs:
                copies(pr)
            for pr in prs:
                quantise(pr)
            for pr in prs:
                multiply(pr - 1)
                drains_and_store(pr - 1)
            first += size
        multiply(15)
        drains_and_store(15)
